import numpy as np
import ml_dtypes


def mxq(x, axis, fmt="e4m3"):
    dtype, down = {"e4m3": (ml_dtypes.float8_e4m3fn, 7), "e5m2": (ml_dtypes.float8_e5m2, 14)}[fmt]
    v = np.moveaxis(np.asarray(x, np.float32).astype(ml_dtypes.bfloat16).astype(np.float64), axis, -1)
    blocks = v.reshape(v.shape[:-1] + (-1, 32))
    amax = np.abs(blocks).max(-1, keepdims=True)
    byte = np.maximum(np.where(amax > 0, np.frexp(amax)[1] - 1 + 127, 0) - down, 1)
    scale = np.exp2(byte - 127.0)
    codes = (blocks / scale).astype(np.float32).astype(dtype).astype(np.float64)
    return np.moveaxis((codes * scale).reshape(v.shape), -1, axis)


WIDE = False


def mx_kscale(k):
    if not WIDE:
        return np.ones(k)
    levels = np.array([10, -10, 5, -5, 0])
    a = np.random.permutation(np.resize(levels, k // 512 * 4)).reshape(k // 512, 4)
    idx = np.arange(k)
    return np.exp2(a[idx // 512, idx % 128 // 32])


BF16 = ml_dtypes.bfloat16


def bf(x):
    return np.asarray(x, np.float32).astype(BF16)


def f64(x):
    return np.asarray(x).astype(np.float64)


B, S, D, E, WINDOW = 2, 512, 1024, 1024, 10
HALF = WINDOW // 2


def setup_inputs():
    s, t = mx_kscale(D), mx_kscale(E)
    return {"x": bf(np.random.standard_normal((B, S, D)) * s),
            "Wq": bf(np.random.standard_normal((E, D)) / np.sqrt(D) / s[None, :] * t[:, None]),
            "bq": bf(np.random.standard_normal(E) * 0.1 * t),
            "k": bf(np.random.standard_normal((B, S, E)) / t)}


def reference(x, Wq, bq, k):
    q = (mxq(f64(x), 2, "e4m3") @ mxq(f64(Wq), 1, "e4m3").T) + f64(bq)
    scores = (mxq(q, 2, "e4m3") @ mxq(f64(k), 2, "e4m3").transpose(0, 2, 1)) / np.sqrt(E)
    i = np.arange(S)[:, None]
    j = np.arange(S)[None, :]
    mask = np.abs(i - j) <= HALF
    scores = np.where(mask[None, :, :], scores, -1e9)
    e = np.exp(scores - scores.max(-1, keepdims=True))
    return e / e.sum(-1, keepdims=True)

@@ -1,0 +1,230 @@
+from contextlib import ExitStack
+
+import concourse.mybir as mybir
+from concourse.masks import make_identity
+
+F32 = mybir.dt.float32
+BF16 = mybir.dt.bfloat16
+U32 = mybir.dt.uint32
+U8 = mybir.dt.uint8
+FP8X4 = mybir.dt.float8_e4m3fn_x4
+ALU = mybir.AluOpType
+ACT = mybir.ActivationFunctionType
+
+B, S, D, E = 2, 512, 1024, 1024
+HALF_WINDOW = 5
+MASKED = -1.0e9
+
+P = 128
+PACK = 4
+K_PASS = P * PACK
+PASSES = D // K_PASS
+ROWS = B * S
+PAIR = 2 * P
+TILES = S // P
+
+KEYS = 256
+BAND = 144
+
+FLOPS = 2 * B * S * D * E + 2 * B * S * S * E
+
+ARRIVALS = (
+    ("x", 0), ("w", 0), ("w", 1), ("w", 2), ("w", 3), ("x", 1), ("k", 0), ("k", 1),
+    ("x", 2), ("x", 3), ("k", 2), ("k", 3),
+)
+LAG = 2
+
+
+def first_key(t):
+    return min(max(t * P - (KEYS - P) // 2, 0), S - KEYS)
+
+
+def first_band_key(t):
+    return min(max(t * P - (BAND - P) // 2, 0), S - BAND)
+
+
+def tile_localattention_pa_kernel(tc, x, Wq, bq, k, out):
+    nc = tc.nc
+    matrices = {"x": x.flatten_outer_dims(), "w": Wq, "k": k.flatten_outer_dims()}
+
+    with ExitStack() as ctx:
+        keep = ctx.enter_context(tc.tile_pool(name="keep", bufs=1))
+        soft = ctx.enter_context(tc.tile_pool(name="soft", bufs=4))
+        turned_pool = ctx.enter_context(tc.psum_pool(name="turned_pool", bufs=3))
+        q_pool = ctx.enter_context(tc.psum_pool(name="q_pool", bufs=3))
+        score_pool = ctx.enter_context(tc.psum_pool(name="score_pool", bufs=2))
+        ctx.enter_context(tc.manual_schedule())
+
+        identity = keep.tile([P, P], F32, name="identity")
+        make_identity(nc, identity[:])
+
+        band_mask = keep.tile([P, TILES, BAND], F32, name="band_mask")
+        nc.gpsimd.memset(band_mask[:], 0.0)
+        for t in range(TILES):
+            ahead = t * P - first_band_key(t)
+            nc.gpsimd.affine_select(
+                out=band_mask[:, t, :], in_=band_mask[:, t, :], compare_op=ALU.is_ge, fill=MASKED,
+                base=ahead + HALF_WINDOW, channel_multiplier=1, pattern=[[-1, BAND]],
+            )
+            nc.gpsimd.affine_select(
+                out=band_mask[:, t, :], in_=band_mask[:, t, :], compare_op=ALU.is_ge, fill=MASKED,
+                base=HALF_WINDOW - ahead, channel_multiplier=-1, pattern=[[1, BAND]],
+            )
+
+        zeros = keep.tile([P, S - BAND], F32, name="zeros")
+        nc.vector.memset(zeros[:], 0.0)
+
+        bias = keep.tile([P, PASSES * 2, 2], BF16, name="bias")
+        nc.scalar.dma_start(out=bias[:], in_=bq.rearrange("(c p e) -> p c e", p=P, e=2))
+        bias_by_pass = bias[:].rearrange("p (g u) e -> p g (u e)", g=PASSES)
+
+        warm = keep.tile([P, 1], F32, name="warm")
+        nc.scalar.activation(out=warm[:], in_=zeros[:, 0:1], func=ACT.Exp)
+
+        raw = {}
+        for name, a in ARRIVALS:
+            raw[(name, a)] = keep.tile([P, 2, D], BF16, name="raw_%s%d" % (name, a))
+            nc.sync.dma_start(
+                out=raw[(name, a)][:].rearrange("p e d -> p (e d)"),
+                in_=matrices[name][a * PAIR : (a + 1) * PAIR, :].rearrange("(p e) d -> p (e d)", e=2),
+            )
+        for b in range(B):
+            for t in range(TILES):
+                rows = slice(t * P, (t + 1) * P)
+                left = first_band_key(t)
+                right = S - BAND - left
+                if left > 0:
+                    nc.sync.dma_start(out=out[b, rows, 0:left], in_=zeros[:, 0:left])
+                if right > 0:
+                    nc.sync.dma_start(out=out[b, rows, S - right : S], in_=zeros[:, 0:right])
+
+        grouped = {}
+        codes = {}
+        scales = {}
+        for name in ("x", "w", "k", "q"):
+            grouped[name] = keep.tile(
+                [P, PASSES, ROWS, PACK], BF16, name="grouped_" + name, align_bytes=64
+            )
+            codes[name] = keep.tile([P, PASSES, ROWS], U32, name="codes_" + name, align_bytes=64)
+            scales[name] = keep.tile([P, PASSES, ROWS], U8, name="scales_" + name, align_bytes=64)
+
+        def turn(name, a):
+            words = raw[(name, a)][:].bitcast(F32)
+            grouped_words = grouped[name][:].bitcast(F32)
+            for g in range(PASSES):
+                turned = turned_pool.tile([P, 2, 2, P], F32, name="turned")
+                for e in range(2):
+                    for u in range(2):
+                        first = (2 * g + u) * P
+                        nc.tensor.transpose(
+                            turned[:, e, u, :], words[:, e, first : first + P], identity[:]
+                        )
+                columns = grouped_words[:, g, a * PAIR : (a + 1) * PAIR, :]
+                if name == "w":
+                    nc.scalar.copy(
+                        out=columns.rearrange("p (e r) u -> p e r u", e=2),
+                        in_=turned[:].rearrange("p e u r -> p e r u"),
+                    )
+                else:
+                    nc.scalar.copy(
+                        out=columns.rearrange("p (r e) u -> p r e u", e=2),
+                        in_=turned[:].rearrange("p e u r -> p r e u"),
+                    )
+
+        def quantise(name, a):
+            columns = slice(a * PAIR, (a + 1) * PAIR)
+            for g in range(PASSES):
+                nc.vector.quantize_mx(
+                    out=codes[name][:, g, columns].bitcast(FP8X4),
+                    scales=scales[name][:, g, columns],
+                    in_=grouped[name][:, g, columns, :].rearrange("p c t -> p (c t)"),
+                )
+
+        def project(a, half):
+            for tokens in (slice(a * PAIR, a * PAIR + P), slice(a * PAIR + P, (a + 1) * PAIR)):
+                q_sum = q_pool.tile([P, PACK, P], F32, name="q_sum")
+                for t in range(PACK):
+                    features = slice((half * PACK + t) * P, (half * PACK + t + 1) * P)
+                    for g in range(PASSES):
+                        nc.tensor.matmul_mx(
+                            out=q_sum[:, t, :],
+                            lhsT=codes["w"][:, g, features].bitcast(FP8X4),
+                            lhsT_scale=scales["w"][:, g, features],
+                            rhs=codes["x"][:, g, tokens].bitcast(FP8X4),
+                            rhs_scale=scales["x"][:, g, tokens],
+                            start=(g == 0),
+                            stop=(g == PASSES - 1),
+                        )
+                nc.vector.tensor_tensor(
+                    out=grouped["q"][:, half, tokens, :],
+                    in0=q_sum[:].rearrange("p t r -> p r t"),
+                    in1=bias_by_pass[:, half, :].unsqueeze(1).to_broadcast([P, P, PACK]),
+                    op=ALU.add,
+                )
+
+        def attend(b):
+            exps = {}
+            sums = {}
+            for t in range(TILES + 1):
+                if t < TILES:
+                    queries = slice(b * S + t * P, b * S + (t + 1) * P)
+                    keys = slice(b * S + first_key(t), b * S + first_key(t) + KEYS)
+                    score = score_pool.tile([P, KEYS], F32, name="score")
+                    for g in range(PASSES):
+                        nc.tensor.matmul_mx(
+                            out=score[:],
+                            lhsT=codes["q"][:, g, queries].bitcast(FP8X4),
+                            lhsT_scale=scales["q"][:, g, queries],
+                            rhs=codes["k"][:, g, keys].bitcast(FP8X4),
+                            rhs_scale=scales["k"][:, g, keys],
+                            start=(g == 0),
+                            stop=(g == PASSES - 1),
+                        )
+                    skip = first_band_key(t) - first_key(t)
+                    masked = soft.tile([P, BAND], F32, name="masked")
+                    nc.vector.scalar_tensor_tensor(
+                        out=masked[:], in0=score[:, skip : skip + BAND], scalar=1.0 / 32.0,
+                        in1=band_mask[:, t, :], op0=ALU.mult, op1=ALU.add,
+                    )
+                    minus_max = soft.tile([P, 1], F32, name="minus_max")
+                    nc.vector.tensor_reduce(
+                        out=minus_max[:], in_=masked[:], axis=mybir.AxisListType.X, op=ALU.max,
+                        negate=True,
+                    )
+                    exps[t] = soft.tile([P, BAND], F32, name="exps")
+                    sums[t] = soft.tile([P, 1], F32, name="sums")
+                    nc.scalar.activation(
+                        out=exps[t][:], in_=masked[:], func=ACT.Exp, bias=minus_max[:], scale=1.0,
+                        accum_out=sums[t][:],
+                    )
+                if t > 0:
+                    done = t - 1
+                    inverse = soft.tile([P, 1], F32, name="inverse")
+                    nc.vector.reciprocal(out=inverse[:], in_=sums[done][:])
+                    weights = soft.tile([P, BAND], F32, name="weights")
+                    nc.scalar.activation(
+                        out=weights[:], in_=exps[done][:], func=ACT.Copy, scale=inverse[:]
+                    )
+                    left = first_band_key(done)
+                    nc.sync.dma_start(
+                        out=out[b, done * P : (done + 1) * P, left : left + BAND], in_=weights[:]
+                    )
+
+        def matmuls_after(name, a):
+            if name == "w" and a % 2 == 1:
+                project(0, a // 2)
+                if a == 3:
+                    quantise("q", 0)
+            if name == "x" and a > 0:
+                project(a, 0)
+                project(a, 1)
+                quantise("q", a)
+            if name == "k" and a % 2 == 1:
+                attend(a // 2)
+
+        for step in range(len(ARRIVALS) + LAG):
+            if step < len(ARRIVALS):
+                turn(*ARRIVALS[step])
+                quantise(*ARRIVALS[step])
+            if step >= LAG:
+                matmuls_after(*ARRIVALS[step - LAG])

@@ -53,7 +53,6 @@ def tile_localattention_pa_kernel(tc, x, Wq, bq, k, out):
         turned_pool = ctx.enter_context(tc.psum_pool(name="turned_pool", bufs=3))
         q_pool = ctx.enter_context(tc.psum_pool(name="q_pool", bufs=3))
         score_pool = ctx.enter_context(tc.psum_pool(name="score_pool", bufs=2))
-        ctx.enter_context(tc.manual_schedule())
 
         identity = keep.tile([P, P], F32, name="identity")
         make_identity(nc, identity[:])

@@ -50,9 +50,7 @@ def tile_localattention_pa_kernel(tc, x, Wq, bq, k, out):
     with ExitStack() as ctx:
         keep = ctx.enter_context(tc.tile_pool(name="keep", bufs=1))
         soft = ctx.enter_context(tc.tile_pool(name="soft", bufs=4))
-        turned_pool = ctx.enter_context(tc.psum_pool(name="turned_pool", bufs=3))
-        q_pool = ctx.enter_context(tc.psum_pool(name="q_pool", bufs=3))
-        score_pool = ctx.enter_context(tc.psum_pool(name="score_pool", bufs=2))
+        banks = ctx.enter_context(tc.psum_pool(name="banks", bufs=8))
 
         identity = keep.tile([P, P], F32, name="identity")
         make_identity(nc, identity[:])
@@ -111,7 +109,7 @@ def tile_localattention_pa_kernel(tc, x, Wq, bq, k, out):
             words = raw[(name, a)][:].bitcast(F32)
             grouped_words = grouped[name][:].bitcast(F32)
             for g in range(PASSES):
-                turned = turned_pool.tile([P, 2, 2, P], F32, name="turned")
+                turned = banks.tile([P, 2, 2, P], F32, name="turned", tag="bank")
                 for e in range(2):
                     for u in range(2):
                         first = (2 * g + u) * P
@@ -141,7 +139,7 @@ def tile_localattention_pa_kernel(tc, x, Wq, bq, k, out):
 
         def project(a, half):
             for tokens in (slice(a * PAIR, a * PAIR + P), slice(a * PAIR + P, (a + 1) * PAIR)):
-                q_sum = q_pool.tile([P, PACK, P], F32, name="q_sum")
+                q_sum = banks.tile([P, PACK, P], F32, name="q_sum", tag="bank")
                 for t in range(PACK):
                     features = slice((half * PACK + t) * P, (half * PACK + t + 1) * P)
                     for g in range(PASSES):
@@ -168,7 +166,7 @@ def tile_localattention_pa_kernel(tc, x, Wq, bq, k, out):
                 if t < TILES:
                     queries = slice(b * S + t * P, b * S + (t + 1) * P)
                     keys = slice(b * S + first_key(t), b * S + first_key(t) + KEYS)
-                    score = score_pool.tile([P, KEYS], F32, name="score")
+                    score = banks.tile([P, KEYS], F32, name="score", tag="bank")
                     for g in range(PASSES):
                         nc.tensor.matmul_mx(
                             out=score[:],

@@ -128,8 +128,8 @@ def tile_localattention_pa_kernel(tc, x, Wq, bq, k, out):
                         in_=turned[:].rearrange("p e u r -> p r e u"),
                     )
 
-        def quantise(name, a):
-            columns = slice(a * PAIR, (a + 1) * PAIR)
+        def quantise(name, a, first=0, rows=PAIR):
+            columns = slice(a * PAIR + first, a * PAIR + first + rows)
             for g in range(PASSES):
                 nc.vector.quantize_mx(
                     out=codes[name][:, g, columns].bitcast(FP8X4),
@@ -137,8 +137,9 @@ def tile_localattention_pa_kernel(tc, x, Wq, bq, k, out):
                     in_=grouped[name][:, g, columns, :].rearrange("p c t -> p (c t)"),
                 )
 
-        def project(a, half):
-            for tokens in (slice(a * PAIR, a * PAIR + P), slice(a * PAIR + P, (a + 1) * PAIR)):
+        def project(a, half, token_tiles=(0, 1)):
+            for j in token_tiles:
+                tokens = slice(a * PAIR + j * P, a * PAIR + (j + 1) * P)
                 q_sum = banks.tile([P, PACK, P], F32, name="q_sum", tag="bank")
                 for t in range(PACK):
                     features = slice((half * PACK + t) * P, (half * PACK + t + 1) * P)
@@ -212,10 +213,15 @@ def tile_localattention_pa_kernel(tc, x, Wq, bq, k, out):
                 project(0, a // 2)
                 if a == 3:
                     quantise("q", 0)
-            if name == "x" and a > 0:
+            if name == "x" and 0 < a < ROWS // PAIR - 1:
                 project(a, 0)
                 project(a, 1)
                 quantise("q", a)
+            if name == "x" and a == ROWS // PAIR - 1:
+                for j in range(2):
+                    project(a, 0, (j,))
+                    project(a, 1, (j,))
+                    quantise("q", a, j * P, P)
             if name == "k" and a % 2 == 1:
                 attend(a // 2)
 

from contextlib import ExitStack

import concourse.mybir as mybir
from concourse.masks import make_identity

F32 = mybir.dt.float32
BF16 = mybir.dt.bfloat16
U32 = mybir.dt.uint32
U8 = mybir.dt.uint8
FP8X4 = mybir.dt.float8_e4m3fn_x4
ALU = mybir.AluOpType
ACT = mybir.ActivationFunctionType

B, S, D, E = 2, 512, 1024, 1024
HALF_WINDOW = 5
MASKED = -1.0e9

P = 128
PACK = 4
K_PASS = P * PACK
PASSES = D // K_PASS
ROWS = B * S
PAIR = 2 * P
TILES = S // P

KEYS = 256
BAND = 144

FLOPS = 2 * B * S * D * E + 2 * B * S * S * E

ARRIVALS = (
    ("x", 0), ("w", 0), ("w", 1), ("w", 2), ("w", 3), ("x", 1), ("k", 0), ("k", 1),
    ("x", 2), ("x", 3), ("k", 2), ("k", 3),
)
LAG = 2


def first_key(t):
    return min(max(t * P - (KEYS - P) // 2, 0), S - KEYS)


def first_band_key(t):
    return min(max(t * P - (BAND - P) // 2, 0), S - BAND)


def tile_localattention_pa_kernel(tc, x, Wq, bq, k, out):
    nc = tc.nc
    matrices = {"x": x.flatten_outer_dims(), "w": Wq, "k": k.flatten_outer_dims()}

    with ExitStack() as ctx:
        keep = ctx.enter_context(tc.tile_pool(name="keep", bufs=1))
        soft = ctx.enter_context(tc.tile_pool(name="soft", bufs=4))
        banks = ctx.enter_context(tc.psum_pool(name="banks", bufs=8))

        identity = keep.tile([P, P], F32, name="identity")
        make_identity(nc, identity[:])

        band_mask = keep.tile([P, TILES, BAND], F32, name="band_mask")
        nc.gpsimd.memset(band_mask[:], 0.0)
        for t in range(TILES):
            ahead = t * P - first_band_key(t)
            nc.gpsimd.affine_select(
                out=band_mask[:, t, :], in_=band_mask[:, t, :], compare_op=ALU.is_ge, fill=MASKED,
                base=ahead + HALF_WINDOW, channel_multiplier=1, pattern=[[-1, BAND]],
            )
            nc.gpsimd.affine_select(
                out=band_mask[:, t, :], in_=band_mask[:, t, :], compare_op=ALU.is_ge, fill=MASKED,
                base=HALF_WINDOW - ahead, channel_multiplier=-1, pattern=[[1, BAND]],
            )

        zeros = keep.tile([P, S - BAND], F32, name="zeros")
        nc.vector.memset(zeros[:], 0.0)

        bias = keep.tile([P, PASSES * 2, 2], BF16, name="bias")
        nc.scalar.dma_start(out=bias[:], in_=bq.rearrange("(c p e) -> p c e", p=P, e=2))
        bias_by_pass = bias[:].rearrange("p (g u) e -> p g (u e)", g=PASSES)

        warm = keep.tile([P, 1], F32, name="warm")
        nc.scalar.activation(out=warm[:], in_=zeros[:, 0:1], func=ACT.Exp)

        raw = {}
        for name, a in ARRIVALS:
            raw[(name, a)] = keep.tile([P, 2, D], BF16, name="raw_%s%d" % (name, a))
            nc.sync.dma_start(
                out=raw[(name, a)][:].rearrange("p e d -> p (e d)"),
                in_=matrices[name][a * PAIR : (a + 1) * PAIR, :].rearrange("(p e) d -> p (e d)", e=2),
            )
        for b in range(B):
            for t in range(TILES):
                rows = slice(t * P, (t + 1) * P)
                left = first_band_key(t)
                right = S - BAND - left
                if left > 0:
                    nc.sync.dma_start(out=out[b, rows, 0:left], in_=zeros[:, 0:left])
                if right > 0:
                    nc.sync.dma_start(out=out[b, rows, S - right : S], in_=zeros[:, 0:right])

        grouped = {}
        codes = {}
        scales = {}
        for name in ("x", "w", "k", "q"):
            grouped[name] = keep.tile(
                [P, PASSES, ROWS, PACK], BF16, name="grouped_" + name, align_bytes=64
            )
            codes[name] = keep.tile([P, PASSES, ROWS], U32, name="codes_" + name, align_bytes=64)
            scales[name] = keep.tile([P, PASSES, ROWS], U8, name="scales_" + name, align_bytes=64)

        def turn(name, a):
            words = raw[(name, a)][:].bitcast(F32)
            grouped_words = grouped[name][:].bitcast(F32)
            for g in range(PASSES):
                turned = banks.tile([P, 2, 2, P], F32, name="turned", tag="bank")
                for e in range(2):
                    for u in range(2):
                        first = (2 * g + u) * P
                        nc.tensor.transpose(
                            turned[:, e, u, :], words[:, e, first : first + P], identity[:]
                        )
                columns = grouped_words[:, g, a * PAIR : (a + 1) * PAIR, :]
                if name == "w":
                    nc.scalar.copy(
                        out=columns.rearrange("p (e r) u -> p e r u", e=2),
                        in_=turned[:].rearrange("p e u r -> p e r u"),
                    )
                else:
                    nc.scalar.copy(
                        out=columns.rearrange("p (r e) u -> p r e u", e=2),
                        in_=turned[:].rearrange("p e u r -> p r e u"),
                    )

        def quantise(name, a, first=0, rows=PAIR):
            columns = slice(a * PAIR + first, a * PAIR + first + rows)
            for g in range(PASSES):
                nc.vector.quantize_mx(
                    out=codes[name][:, g, columns].bitcast(FP8X4),
                    scales=scales[name][:, g, columns],
                    in_=grouped[name][:, g, columns, :].rearrange("p c t -> p (c t)"),
                )

        def project(a, half, token_tiles=(0, 1)):
            for j in token_tiles:
                tokens = slice(a * PAIR + j * P, a * PAIR + (j + 1) * P)
                q_sum = banks.tile([P, PACK, P], F32, name="q_sum", tag="bank")
                for t in range(PACK):
                    features = slice((half * PACK + t) * P, (half * PACK + t + 1) * P)
                    for g in range(PASSES):
                        nc.tensor.matmul_mx(
                            out=q_sum[:, t, :],
                            lhsT=codes["w"][:, g, features].bitcast(FP8X4),
                            lhsT_scale=scales["w"][:, g, features],
                            rhs=codes["x"][:, g, tokens].bitcast(FP8X4),
                            rhs_scale=scales["x"][:, g, tokens],
                            start=(g == 0),
                            stop=(g == PASSES - 1),
                        )
                nc.vector.tensor_tensor(
                    out=grouped["q"][:, half, tokens, :],
                    in0=q_sum[:].rearrange("p t r -> p r t"),
                    in1=bias_by_pass[:, half, :].unsqueeze(1).to_broadcast([P, P, PACK]),
                    op=ALU.add,
                )

        def attend(b):
            exps = {}
            sums = {}
            for t in range(TILES + 1):
                if t < TILES:
                    queries = slice(b * S + t * P, b * S + (t + 1) * P)
                    keys = slice(b * S + first_key(t), b * S + first_key(t) + KEYS)
                    score = banks.tile([P, KEYS], F32, name="score", tag="bank")
                    for g in range(PASSES):
                        nc.tensor.matmul_mx(
                            out=score[:],
                            lhsT=codes["q"][:, g, queries].bitcast(FP8X4),
                            lhsT_scale=scales["q"][:, g, queries],
                            rhs=codes["k"][:, g, keys].bitcast(FP8X4),
                            rhs_scale=scales["k"][:, g, keys],
                            start=(g == 0),
                            stop=(g == PASSES - 1),
                        )
                    skip = first_band_key(t) - first_key(t)
                    masked = soft.tile([P, BAND], F32, name="masked")
                    nc.vector.scalar_tensor_tensor(
                        out=masked[:], in0=score[:, skip : skip + BAND], scalar=1.0 / 32.0,
                        in1=band_mask[:, t, :], op0=ALU.mult, op1=ALU.add,
                    )
                    minus_max = soft.tile([P, 1], F32, name="minus_max")
                    nc.vector.tensor_reduce(
                        out=minus_max[:], in_=masked[:], axis=mybir.AxisListType.X, op=ALU.max,
                        negate=True,
                    )
                    exps[t] = soft.tile([P, BAND], F32, name="exps")
                    sums[t] = soft.tile([P, 1], F32, name="sums")
                    nc.scalar.activation(
                        out=exps[t][:], in_=masked[:], func=ACT.Exp, bias=minus_max[:], scale=1.0,
                        accum_out=sums[t][:],
                    )
                if t > 0:
                    done = t - 1
                    inverse = soft.tile([P, 1], F32, name="inverse")
                    nc.vector.reciprocal(out=inverse[:], in_=sums[done][:])
                    weights = soft.tile([P, BAND], F32, name="weights")
                    nc.scalar.activation(
                        out=weights[:], in_=exps[done][:], func=ACT.Copy, scale=inverse[:]
                    )
                    left = first_band_key(done)
                    nc.sync.dma_start(
                        out=out[b, done * P : (done + 1) * P, left : left + BAND], in_=weights[:]
                    )

        def matmuls_after(name, a):
            if name == "w" and a % 2 == 1:
                project(0, a // 2)
                if a == 3:
                    quantise("q", 0)
            if name == "x" and 0 < a < ROWS // PAIR - 1:
                project(a, 0)
                project(a, 1)
                quantise("q", a)
            if name == "x" and a == ROWS // PAIR - 1:
                for j in range(2):
                    project(a, 0, (j,))
                    project(a, 1, (j,))
                    quantise("q", a, j * P, P)
            if name == "k" and a % 2 == 1:
                attend(a // 2)

        for step in range(len(ARRIVALS) + LAG):
            if step < len(ARRIVALS):
                turn(*ARRIVALS[step])
                quantise(*ARRIVALS[step])
            if step >= LAG:
                matmuls_after(*ARRIVALS[step - LAG])
